import numpy as np
import ml_dtypes


def mxq(x, axis, fmt="e4m3"):
    dtype, down = {"e4m3": (ml_dtypes.float8_e4m3fn, 7), "e5m2": (ml_dtypes.float8_e5m2, 14)}[fmt]
    v = np.moveaxis(np.asarray(x, np.float32).astype(ml_dtypes.bfloat16).astype(np.float64), axis, -1)
    blocks = v.reshape(v.shape[:-1] + (-1, 32))
    amax = np.abs(blocks).max(-1, keepdims=True)
    byte = np.maximum(np.where(amax > 0, np.frexp(amax)[1] - 1 + 127, 0) - down, 1)
    scale = np.exp2(byte - 127.0)
    codes = (blocks / scale).astype(np.float32).astype(dtype).astype(np.float64)
    return np.moveaxis((codes * scale).reshape(v.shape), -1, axis)


WIDE = False


def mx_kscale(k):
    if not WIDE:
        return np.ones(k)
    levels = np.array([10, -10, 5, -5, 0])
    a = np.random.permutation(np.resize(levels, k // 512 * 4)).reshape(k // 512, 4)
    idx = np.arange(k)
    return np.exp2(a[idx // 512, idx % 128 // 32])


BF16 = ml_dtypes.bfloat16


def bf(x):
    return np.asarray(x, np.float32).astype(BF16)


def f64(x):
    return np.asarray(x).astype(np.float64)


E2M1 = np.array([0.0, 0.5, 1.0, 1.5, 2.0, 3.0, 4.0, 6.0, -0.0, -0.5, -1.0, -1.5, -2.0, -3.0, -4.0, -6.0])


def pack_weight(w, fmt):
    k, n = w.shape
    w = f64(bf(w)).reshape(k // 32, 32, n)
    amax = np.abs(w).max(1)
    if fmt == "e4m3":
        byte = np.frexp(amax)[1] - 1 + 127 - 7
    else:
        mant, ex = np.frexp(amax / 6.0)
        byte = np.where(mant > 0.5, ex, ex - 1) + 127
    byte = np.clip(np.where(amax > 0, byte, 1), 1, 254)
    scaled = (w * np.exp2(127.0 - byte)[:, None, :]).reshape(k, n).astype(np.float32)
    by_word = np.ascontiguousarray(scaled.reshape(k // 512, 128, 4, n).transpose(0, 1, 3, 2))
    if fmt == "e4m3":
        words = by_word.astype(ml_dtypes.float8_e4m3fn).view(np.uint8)
    else:
        c = by_word.astype(ml_dtypes.float4_e2m1fn).view(np.uint8) & 0xF
        words = c[..., 0::2] | (c[..., 1::2] << 4)
    return np.ascontiguousarray(words), np.ascontiguousarray(byte.astype(np.uint8).reshape(k // 512, 16, n))


def unpack_weight(words, scales, fmt):
    g, p, n, _ = words.shape
    if fmt == "e4m3":
        vals = np.ascontiguousarray(words).view(ml_dtypes.float8_e4m3fn).astype(np.float64)
    else:
        nib = np.empty((g, p, n, 4), np.uint8)
        nib[..., 0::2] = words & 0xF
        nib[..., 1::2] = words >> 4
        vals = E2M1[nib]
    vals = vals * np.repeat(np.exp2(scales.astype(np.float64) - 127.0), 8, axis=1)[..., None]
    return vals.transpose(0, 1, 3, 2).reshape(g * 512, n)

def pack4(w):
    words, scales = pack_weight(w, "e2m1")
    return words.reshape(words.shape[0], 128, -1), scales


def unpack4(words, scales):
    return unpack_weight(words.reshape(words.shape[0], 128, -1, 2), scales, "e2m1")


B, IN, H, G, GA, GB = 256, 16384, 1024, 6, 4, 2
EPS = 1e-5


def layer_norm(v, g, b):
    mu = v.mean(-1, keepdims=True)
    var = np.square(v - mu).mean(-1, keepdims=True)
    return (v - mu) / np.sqrt(var + EPS) * g + b


def sigmoid(v):
    return 1.0 / (1.0 + np.exp(-v))


def setup_inputs():
    s = mx_kscale(IN)
    x = bf(np.random.standard_normal((B, IN)) * s)
    h = bf(np.random.standard_normal((B, H)))
    c = bf(np.tanh(1.4 * np.random.standard_normal((B, H))))
    W_u_words, W_u_scales = pack4((np.random.standard_normal((H, H)) / np.sqrt(H)).T)
    U_u_words, U_u_scales = pack4((np.random.standard_normal((H, IN)) / np.sqrt(IN) / s).T)
    ln_gamma = bf(1.0 + 0.1 * np.random.standard_normal((GB, H)))
    ln_beta = bf(0.2 * np.random.standard_normal((GB, H)))
    return {"x": x,
            "h": h,
            "c": c,
            "W_u_words": W_u_words,
            "W_u_scales": W_u_scales,
            "U_u_words": U_u_words,
            "U_u_scales": U_u_scales,
            "ln_gamma": ln_gamma,
            "ln_beta": ln_beta}


def reference(x, h, c, W_u_words, W_u_scales, U_u_words, U_u_scales, ln_gamma, ln_beta):
    g_uh, g_ux = f64(ln_gamma)
    b_uh, b_ux = f64(ln_beta)
    hf = f64(h)
    u = sigmoid(layer_norm(mxq(hf, 1, "e4m3") @ unpack4(W_u_words, W_u_scales), g_uh, b_uh)
                + layer_norm(mxq(f64(x), 1, "e4m3") @ unpack4(U_u_words, U_u_scales), g_ux, b_ux))
    return (1.0 - u) * hf + u * f64(c)

@@ -1,0 +1,313 @@
+from contextlib import ExitStack
+
+import concourse.mybir as mybir
+from concourse.masks import make_identity
+
+F32 = mybir.dt.float32
+BF16 = mybir.dt.bfloat16
+U8 = mybir.dt.uint8
+U32 = mybir.dt.uint32
+I32 = mybir.dt.int32
+FP8X4 = mybir.dt.float8_e4m3fn_x4
+FP4X4 = mybir.dt.float4_e2m1fn_x4
+ALU = mybir.AluOpType
+ACT = mybir.ActivationFunctionType
+
+P = 128
+ROWS = 256
+ROW_TILES = ROWS // P
+IN = 16384
+H = 1024
+EPS = 1e-5
+
+K_PASS = 512
+WORDS = K_PASS // 2
+HALF = 512
+HALVES = H // HALF
+UNIT = 4
+BANK_TURNS = 4
+UNIT_BANKS = 2 * UNIT // BANK_TURNS
+H_GROUPS = H // K_PASS
+CHUNKS = IN // (UNIT * K_PASS)
+LAG_CHUNKS = 2
+X_BUFFERS = 6
+STEP_BUFFERS = 4
+
+FLOPS = 2 * ROWS * (IN + H) * H
+
+H_UNIT = ("h", 0, 0)
+
+
+def plan_steps():
+    steps = [[H_UNIT]]
+    for c in range(CHUNKS):
+        behind = [("x", 1, c - LAG_CHUNKS)] if c >= LAG_CHUNKS else []
+        steps.append(behind + [("x", 0, c)])
+    rest = [("x", 1, c) for c in range(CHUNKS - LAG_CHUNKS, CHUNKS)]
+    for first in range(0, LAG_CHUNKS, 2):
+        steps.append(rest[first : first + 2])
+    return steps
+
+
+def tile_layernormgrucell_pb_k_kernel(
+    tc, x, h, c, W_u_words, W_u_scales, U_u_words, U_u_scales, ln_gamma, ln_beta, out
+):
+    nc = tc.nc
+    steps = plan_steps()
+    n_steps = len(steps)
+    n_spread = 3
+    assert all(len(steps[s]) == 1 for s in range(n_spread))
+
+    with ExitStack() as ctx:
+        keep = ctx.enter_context(tc.tile_pool(name="keep", bufs=1))
+        x_pool = ctx.enter_context(tc.tile_pool(name="x_pool", bufs=X_BUFFERS))
+        step_pool = ctx.enter_context(tc.tile_pool(name="step_pool", bufs=STEP_BUFFERS))
+        sum_pool = ctx.enter_context(tc.psum_pool(name="sum_pool", bufs=1))
+        turn_pool = ctx.enter_context(tc.psum_pool(name="turn_pool", bufs=2 * UNIT_BANKS))
+        ctx.enter_context(tc.manual_schedule())
+
+        h_sb = keep.tile([P, ROW_TILES, H], BF16, name="h_sb")
+        c_sb = keep.tile([P, ROW_TILES, H], BF16, name="c_sb")
+        w_words = keep.tile([P, H_GROUPS, 2 * H], U8, name="w_words", align_bytes=64)
+        w_plane = keep.tile([P, H_GROUPS, H], U8, name="w_plane", align_bytes=64)
+        u_words = [
+            keep.tile([P, UNIT, 2 * H], U8, name="u_words%d" % k, align_bytes=64) for k in range(CHUNKS)
+        ]
+        u_plane = [
+            keep.tile([P, UNIT, H], U8, name="u_plane%d" % k, align_bytes=64) for k in range(CHUNKS)
+        ]
+        identity = keep.tile([P, P], F32, name="identity")
+        ones = keep.tile([P, P], BF16, name="ones")
+        minus_half = keep.tile([P, 1], F32, name="minus_half")
+        table_warm = keep.tile([P, 1], F32, name="table_warm")
+        spread_src = keep.tile([P, n_spread, H], BF16, name="spread_src")
+        spread = keep.tile([P, n_spread, H], F32, name="spread")
+        hidden_term = [keep.tile([P, H], F32, name="hidden_term%d" % t) for t in range(ROW_TILES)]
+        c_minus_h = keep.tile([P, ROW_TILES, H], F32, name="c_minus_h")
+        result = [keep.tile([P, H], F32, name="result%d" % t) for t in range(ROW_TILES)]
+
+        def zero_plane(plane):
+            nc.vector.memset(plane[:].bitcast(I32), 0)
+
+        raw = {}
+
+        def load_activations(step):
+            for unit in steps[step]:
+                if unit == H_UNIT:
+                    nc.sync.dma_start(out=h_sb[:], in_=h.rearrange("(t p) k -> p t k", p=P))
+                    raw[unit] = h_sb[:].rearrange("p t k -> p (t k)")
+                else:
+                    t, chunk = unit[1], unit[2]
+                    x_raw = x_pool.tile([P, UNIT * K_PASS], BF16, name="x_raw")
+                    nc.sync.dma_start(
+                        out=x_raw[:],
+                        in_=x[t * P : (t + 1) * P, chunk * UNIT * K_PASS : (chunk + 1) * UNIT * K_PASS],
+                    )
+                    raw[unit] = x_raw[:]
+
+        def load_quantised(words, plane, words_dram, scales_dram):
+            for low_q in range(2):
+                for r in range(4):
+                    nc.sync.dma_start(
+                        out=plane[32 * low_q + r : P : 64, :, :].bitcast(I32),
+                        in_=scales_dram[:, 4 * low_q + r : 16 : 8, :].rearrange("g q n -> q g n"),
+                    )
+            nc.sync.dma_start(out=words[:].bitcast(I32), in_=words_dram.rearrange("g p b -> p g b"))
+
+        w_words_dram = W_u_words.bitcast(I32)
+        w_scales_dram = W_u_scales.bitcast(I32)
+        u_words_dram = U_u_words.bitcast(I32)
+        u_scales_dram = U_u_scales.bitcast(I32)
+
+        def load_weights(step):
+            for unit in steps[step]:
+                if unit == H_UNIT:
+                    nc.sync.dma_start(out=spread_src[0:1, 0:2, :], in_=ln_gamma.unsqueeze(0))
+                    nc.sync.dma_start(out=spread_src[0:2, 2, :], in_=ln_beta)
+                    load_quantised(w_words, w_plane, w_words_dram, w_scales_dram)
+                elif unit[1] == 0:
+                    chunk = unit[2]
+                    groups = slice(chunk * UNIT, (chunk + 1) * UNIT)
+                    load_quantised(
+                        u_words[chunk], u_plane[chunk], u_words_dram[groups], u_scales_dram[groups]
+                    )
+
+        sorted_words = {}
+        turned = {}
+        spread_banks = {}
+        codes = {}
+        code_scales = {}
+
+        def sort_words(step):
+            for unit in steps[step]:
+                by_parity = step_pool.tile([P, UNIT, 2, P], F32, name="by_parity")
+                nc.vector.tensor_copy(
+                    out=by_parity[:],
+                    in_=raw[unit].bitcast(F32).rearrange("p (k w u) -> p k u w", k=UNIT, u=2),
+                )
+                sorted_words[unit] = by_parity
+
+        def transpose(step):
+            for unit in steps[step]:
+                turned[unit] = []
+                for bank in range(UNIT_BANKS):
+                    turn = turn_pool.tile([P, BANK_TURNS, P], F32, name="turn")
+                    for q in range(BANK_TURNS):
+                        operand = (bank * BANK_TURNS + q) // 2
+                        nc.tensor.transpose(
+                            out=turn[:, q, :], in_=sorted_words[unit][:, operand, q % 2, :], identity=identity[:]
+                        )
+                    turned[unit].append(turn)
+            if step < n_spread:
+                spread_banks[step] = []
+                for half in range(HALVES):
+                    turn = turn_pool.tile([P, HALF], F32, name="turn")
+                    nc.tensor.matmul(
+                        out=turn[:],
+                        lhsT=ones[:],
+                        rhs=spread_src[:, step, half * HALF : (half + 1) * HALF],
+                        start=True,
+                        stop=True,
+                    )
+                    spread_banks[step].append(turn)
+
+        def regroup_and_quantise(step):
+            grouped = {}
+            for unit in steps[step]:
+                grouped[unit] = step_pool.tile([P, UNIT * K_PASS], BF16, name="grouped", align_bytes=64)
+                as_words = grouped[unit][:].bitcast(F32).rearrange("p (k r u) -> p k r u", k=UNIT, u=2)
+                per_bank = BANK_TURNS // 2
+                for bank in range(UNIT_BANKS):
+                    nc.scalar.copy(
+                        out=as_words[:, bank * per_bank : (bank + 1) * per_bank, :, :],
+                        in_=turned[unit][bank][:].rearrange("p (k u) r -> p k r u", u=2),
+                    )
+            if step < n_spread:
+                for half in range(HALVES):
+                    nc.scalar.copy(
+                        out=spread[:, step, half * HALF : (half + 1) * HALF], in_=spread_banks[step][half][:]
+                    )
+            for unit in steps[step]:
+                codes[unit] = step_pool.tile([P, UNIT * P], U32, name="codes", align_bytes=64)
+                code_scales[unit] = step_pool.tile([P, UNIT * P], U8, name="code_scales", align_bytes=64)
+                nc.vector.quantize_mx(
+                    out=codes[unit][:].bitcast(FP8X4), scales=code_scales[unit][:], in_=grouped[unit][:]
+                )
+
+        sums = {}
+
+        def open_sums(name, t):
+            sums[(name, t)] = [
+                sum_pool.tile([P, HALF], F32, name="sum_%s%d%d" % (name, t, half), tag="sum%d%d" % (t, half))
+                for half in range(HALVES)
+            ]
+
+        def multiply(step):
+            for unit in steps[step]:
+                for k in range(UNIT):
+                    if unit == H_UNIT:
+                        t, group, last_group = k // H_GROUPS, k % H_GROUPS, H_GROUPS - 1
+                        words, plane = w_words[:, group, :], w_plane[:, group, :]
+                    else:
+                        t, group, last_group = unit[1], unit[2] * UNIT + k, CHUNKS * UNIT - 1
+                        words, plane = u_words[unit[2]][:, k, :], u_plane[unit[2]][:, k, :]
+                    if group == 0:
+                        open_sums(unit[0], t)
+                    for half in range(HALVES):
+                        nc.tensor.matmul_mx(
+                            out=sums[(unit[0], t)][half][:],
+                            lhsT=codes[unit][:, k * P : (k + 1) * P].bitcast(FP8X4),
+                            lhsT_scale=code_scales[unit][:, k * P : (k + 1) * P],
+                            rhs=words[:, half * 2 * HALF : (half + 1) * 2 * HALF].bitcast(FP4X4),
+                            rhs_scale=plane[:, half * HALF : (half + 1) * HALF],
+                            start=(group == 0),
+                            stop=(group == last_group),
+                        )
+
+        def halves_of(tile_ap):
+            return [tile_ap[:, half * HALF : (half + 1) * HALF] for half in range(HALVES)]
+
+        def norm_scale_add(dst, src, gamma, addend, name):
+            stats = keep.tile([P, HALVES, 6], F32, name="stats_" + name)
+            mean_var = keep.tile([P, 2], F32, name="mean_var_" + name)
+            var_eps = keep.tile([P, 1], F32, name="var_eps_" + name)
+            inv_std = keep.tile([P, 1], F32, name="inv_std_" + name)
+            for half in range(HALVES):
+                nc.vector.bn_stats(out=stats[:, half, :], in_=src[half])
+            nc.vector.bn_aggr(out=mean_var[:], in_=stats[:].rearrange("p a s -> p (a s)"))
+            nc.vector.tensor_scalar_add(out=var_eps[:], in0=mean_var[:, 1:2], scalar1=EPS)
+            nc.gpsimd.tensor_tensor(out=inv_std[:], in0=var_eps[:], in1=minus_half[:], op=ALU.pow)
+            for half in range(HALVES):
+                nc.vector.scalar_tensor_tensor(
+                    out=dst[half], in0=src[half], scalar=mean_var[:, 0:1], in1=gamma[half],
+                    op0=ALU.subtract, op1=ALU.mult,
+                )
+            for half in range(HALVES):
+                nc.vector.scalar_tensor_tensor(
+                    out=dst[half], in0=dst[half], scalar=inv_std[:], in1=addend[half],
+                    op0=ALU.mult, op1=ALU.add,
+                )
+
+        def finish(t):
+            res = halves_of(result[t])
+            norm_scale_add(
+                res, [s[:] for s in sums[("x", t)]], halves_of(spread[:, 1, :]), halves_of(hidden_term[t]),
+                "x%d" % t,
+            )
+            for half in range(HALVES):
+                nc.scalar.activation(out=res[half], in_=res[half], func=ACT.Sigmoid)
+            for half in range(HALVES):
+                nc.vector.tensor_mul(out=res[half], in0=res[half], in1=halves_of(c_minus_h[:, t, :])[half])
+            for half in range(HALVES):
+                nc.vector.tensor_add(out=res[half], in0=res[half], in1=halves_of(h_sb[:, t, :])[half])
+                nc.sync.dma_start(
+                    out=out[t * P : (t + 1) * P, half * HALF : (half + 1) * HALF], in_=res[half]
+                )
+
+        early_planes = CHUNKS // 2
+        nc.vector.memset(spread_src[:].bitcast(I32), 0)
+        zero_plane(w_plane)
+        for chunk in range(early_planes):
+            zero_plane(u_plane[chunk])
+        nc.gpsimd.memset(minus_half[:], -0.5)
+        make_identity(nc, identity[:])
+        nc.gpsimd.memset(ones[:], 1.0)
+        nc.scalar.activation(out=table_warm[:], in_=minus_half[:], func=ACT.Sigmoid)
+
+        load_activations(0)
+        load_activations(1)
+        load_weights(0)
+        load_activations(2)
+        load_weights(1)
+        sort_words(0)
+        for chunk in range(early_planes, CHUNKS):
+            zero_plane(u_plane[chunk])
+
+        first_norm_step = n_spread - 1
+        for i in range(-1, n_steps):
+            if i + 4 < n_steps:
+                load_activations(i + 4)
+            if i + 3 < n_steps:
+                load_weights(i + 3)
+            if i + 3 == n_steps - 1:
+                nc.sync.dma_start(out=c_sb[:], in_=c.rearrange("(t p) k -> p t k", p=P))
+            if i + 1 < n_steps:
+                transpose(i + 1)
+                regroup_and_quantise(i + 1)
+            if i + 2 < n_steps:
+                sort_words(i + 2)
+            if i >= 0:
+                multiply(i)
+            if i == 0:
+                for t in range(ROW_TILES):
+                    for half in range(HALVES):
+                        nc.scalar.copy(out=halves_of(hidden_term[t])[half], in_=sums[("h", t)][half][:])
+            if 0 <= i - first_norm_step < ROW_TILES:
+                t = i - first_norm_step
+                term = halves_of(hidden_term[t])
+                norm_scale_add(term, term, halves_of(spread[:, 0, :]), halves_of(spread[:, 2, :]), "h%d" % t)
+            if i == CHUNKS:
+                nc.vector.tensor_sub(out=c_minus_h[:], in0=c_sb[:], in1=h_sb[:])
+                finish(0)
+            if i == n_steps - 1:
+                finish(1)

@@ -30,6 +30,8 @@ UNIT_BANKS = 2 * UNIT // BANK_TURNS
 H_GROUPS = H // K_PASS
 CHUNKS = IN // (UNIT * K_PASS)
 LAG_CHUNKS = 2
+RUN_CHUNKS = 2
+RUNS = CHUNKS // RUN_CHUNKS
 X_BUFFERS = 6
 STEP_BUFFERS = 4
 
@@ -74,7 +76,7 @@ def tile_layernormgrucell_pb_k_kernel(
             keep.tile([P, UNIT, 2 * H], U8, name="u_words%d" % k, align_bytes=64) for k in range(CHUNKS)
         ]
         u_plane = [
-            keep.tile([P, UNIT, H], U8, name="u_plane%d" % k, align_bytes=64) for k in range(CHUNKS)
+            keep.tile([P, RUN_CHUNKS * UNIT, H], U8, name="u_plane%d" % k, align_bytes=64) for k in range(RUNS)
         ]
         identity = keep.tile([P, P], F32, name="identity")
         ones = keep.tile([P, P], BF16, name="ones")
@@ -105,31 +107,37 @@ def tile_layernormgrucell_pb_k_kernel(
                     )
                     raw[unit] = x_raw[:]
 
-        def load_quantised(words, plane, words_dram, scales_dram):
+        def load_plane(plane, scales_dram):
             for low_q in range(2):
                 for r in range(4):
                     nc.sync.dma_start(
                         out=plane[32 * low_q + r : P : 64, :, :].bitcast(I32),
                         in_=scales_dram[:, 4 * low_q + r : 16 : 8, :].rearrange("g q n -> q g n"),
                     )
-            nc.sync.dma_start(out=words[:].bitcast(I32), in_=words_dram.rearrange("g p b -> p g b"))
 
         w_words_dram = W_u_words.bitcast(I32)
         w_scales_dram = W_u_scales.bitcast(I32)
         u_words_dram = U_u_words.bitcast(I32)
         u_scales_dram = U_u_scales.bitcast(I32)
 
-        def load_weights(step):
+        def load_scales(step):
             for unit in steps[step]:
                 if unit == H_UNIT:
-                    nc.sync.dma_start(out=spread_src[0:1, 0:2, :], in_=ln_gamma.unsqueeze(0))
-                    nc.sync.dma_start(out=spread_src[0:2, 2, :], in_=ln_beta)
-                    load_quantised(w_words, w_plane, w_words_dram, w_scales_dram)
+                    load_plane(w_plane, w_scales_dram)
+                elif unit[1] == 0 and unit[2] % RUN_CHUNKS == 0:
+                    run = unit[2] // RUN_CHUNKS
+                    groups = slice(run * RUN_CHUNKS * UNIT, (run + 1) * RUN_CHUNKS * UNIT)
+                    load_plane(u_plane[run], u_scales_dram[groups])
+
+        def load_words(step):
+            for unit in steps[step]:
+                if unit == H_UNIT:
+                    nc.sync.dma_start(out=w_words[:].bitcast(I32), in_=w_words_dram.rearrange("g p b -> p g b"))
                 elif unit[1] == 0:
-                    chunk = unit[2]
-                    groups = slice(chunk * UNIT, (chunk + 1) * UNIT)
-                    load_quantised(
-                        u_words[chunk], u_plane[chunk], u_words_dram[groups], u_scales_dram[groups]
+                    groups = slice(unit[2] * UNIT, (unit[2] + 1) * UNIT)
+                    nc.sync.dma_start(
+                        out=u_words[unit[2]][:].bitcast(I32),
+                        in_=u_words_dram[groups].rearrange("g p b -> p g b"),
                     )
 
         sorted_words = {}
@@ -210,7 +218,8 @@ def tile_layernormgrucell_pb_k_kernel(
                         words, plane = w_words[:, group, :], w_plane[:, group, :]
                     else:
                         t, group, last_group = unit[1], unit[2] * UNIT + k, CHUNKS * UNIT - 1
-                        words, plane = u_words[unit[2]][:, k, :], u_plane[unit[2]][:, k, :]
+                        words = u_words[unit[2]][:, k, :]
+                        plane = u_plane[unit[2] // RUN_CHUNKS][:, group % (RUN_CHUNKS * UNIT), :]
                     if group == 0:
                         open_sums(unit[0], t)
                     for half in range(HALVES):
@@ -264,11 +273,11 @@ def tile_layernormgrucell_pb_k_kernel(
                     out=out[t * P : (t + 1) * P, half * HALF : (half + 1) * HALF], in_=res[half]
                 )
 
-        early_planes = CHUNKS // 2
+        early_planes = RUNS // 2
         nc.vector.memset(spread_src[:].bitcast(I32), 0)
         zero_plane(w_plane)
-        for chunk in range(early_planes):
-            zero_plane(u_plane[chunk])
+        for run in range(early_planes):
+            zero_plane(u_plane[run])
         nc.gpsimd.memset(minus_half[:], -0.5)
         make_identity(nc, identity[:])
         nc.gpsimd.memset(ones[:], 1.0)
@@ -276,19 +285,24 @@ def tile_layernormgrucell_pb_k_kernel(
 
         load_activations(0)
         load_activations(1)
-        load_weights(0)
+        nc.sync.dma_start(out=spread_src[0:1, 0:2, :], in_=ln_gamma.unsqueeze(0))
+        nc.sync.dma_start(out=spread_src[0:2, 2, :], in_=ln_beta)
+        load_scales(0)
+        load_scales(1)
+        load_words(0)
         load_activations(2)
-        load_weights(1)
+        load_words(1)
         sort_words(0)
-        for chunk in range(early_planes, CHUNKS):
-            zero_plane(u_plane[chunk])
+        for run in range(early_planes, RUNS):
+            zero_plane(u_plane[run])
 
         first_norm_step = n_spread - 1
         for i in range(-1, n_steps):
             if i + 4 < n_steps:
                 load_activations(i + 4)
             if i + 3 < n_steps:
-                load_weights(i + 3)
+                load_scales(i + 3)
+                load_words(i + 3)
             if i + 3 == n_steps - 1:
                 nc.sync.dma_start(out=c_sb[:], in_=c.rearrange("(t p) k -> p t k", p=P))
             if i + 1 < n_steps:

@@ -44,7 +44,7 @@ def plan_steps():
     steps = [[H_UNIT]]
     for c in range(CHUNKS):
         behind = [("x", 1, c - LAG_CHUNKS)] if c >= LAG_CHUNKS else []
-        steps.append(behind + [("x", 0, c)])
+        steps.append([("x", 0, c)] + behind)
     rest = [("x", 1, c) for c in range(CHUNKS - LAG_CHUNKS, CHUNKS)]
     for first in range(0, LAG_CHUNKS, 2):
         steps.append(rest[first : first + 2])
@@ -211,18 +211,18 @@ def tile_layernormgrucell_pb_k_kernel(
             ]
 
         def multiply(step):
-            for unit in steps[step]:
-                for k in range(UNIT):
-                    if unit == H_UNIT:
-                        t, group, last_group = k // H_GROUPS, k % H_GROUPS, H_GROUPS - 1
-                        words, plane = w_words[:, group, :], w_plane[:, group, :]
-                    else:
-                        t, group, last_group = unit[1], unit[2] * UNIT + k, CHUNKS * UNIT - 1
-                        words = u_words[unit[2]][:, k, :]
-                        plane = u_plane[unit[2] // RUN_CHUNKS][:, group % (RUN_CHUNKS * UNIT), :]
-                    if group == 0:
-                        open_sums(unit[0], t)
-                    for half in range(HALVES):
+            for half in range(HALVES):
+                for unit in steps[step]:
+                    for k in range(UNIT):
+                        if unit == H_UNIT:
+                            t, group, last_group = k // H_GROUPS, k % H_GROUPS, H_GROUPS - 1
+                            words, plane = w_words[:, group, :], w_plane[:, group, :]
+                        else:
+                            t, group, last_group = unit[1], unit[2] * UNIT + k, CHUNKS * UNIT - 1
+                            words = u_words[unit[2]][:, k, :]
+                            plane = u_plane[unit[2] // RUN_CHUNKS][:, group % (RUN_CHUNKS * UNIT), :]
+                        if group == 0 and half == 0:
+                            open_sums(unit[0], t)
                         nc.tensor.matmul_mx(
                             out=sums[(unit[0], t)][half][:],
                             lhsT=codes[unit][:, k * P : (k + 1) * P].bitcast(FP8X4),
@@ -273,12 +273,10 @@ def tile_layernormgrucell_pb_k_kernel(
                     out=out[t * P : (t + 1) * P, half * HALF : (half + 1) * HALF], in_=res[half]
                 )
 
-        early_planes = RUNS // 2
-        nc.vector.memset(spread_src[:].bitcast(I32), 0)
         zero_plane(w_plane)
-        for run in range(early_planes):
-            zero_plane(u_plane[run])
+        zero_plane(u_plane[0])
         nc.gpsimd.memset(minus_half[:], -0.5)
+        nc.gpsimd.memset(spread_src[:].bitcast(F32), 0.0)
         make_identity(nc, identity[:])
         nc.gpsimd.memset(ones[:], 1.0)
         nc.scalar.activation(out=table_warm[:], in_=minus_half[:], func=ACT.Sigmoid)
@@ -293,35 +291,37 @@ def tile_layernormgrucell_pb_k_kernel(
         load_activations(2)
         load_words(1)
         sort_words(0)
-        for run in range(early_planes, RUNS):
-            zero_plane(u_plane[run])
 
         first_norm_step = n_spread - 1
+        blend_step = n_steps // 2
         for i in range(-1, n_steps):
             if i + 4 < n_steps:
                 load_activations(i + 4)
             if i + 3 < n_steps:
                 load_scales(i + 3)
                 load_words(i + 3)
-            if i + 3 == n_steps - 1:
+            if i + 3 == blend_step:
                 nc.sync.dma_start(out=c_sb[:], in_=c.rearrange("(t p) k -> p t k", p=P))
             if i + 1 < n_steps:
                 transpose(i + 1)
                 regroup_and_quantise(i + 1)
             if i + 2 < n_steps:
                 sort_words(i + 2)
+            if 1 <= i + 2 < RUNS:
+                zero_plane(u_plane[i + 2])
             if i >= 0:
                 multiply(i)
             if i == 0:
-                for t in range(ROW_TILES):
-                    for half in range(HALVES):
+                for half in range(HALVES):
+                    for t in range(ROW_TILES):
                         nc.scalar.copy(out=halves_of(hidden_term[t])[half], in_=sums[("h", t)][half][:])
             if 0 <= i - first_norm_step < ROW_TILES:
                 t = i - first_norm_step
                 term = halves_of(hidden_term[t])
                 norm_scale_add(term, term, halves_of(spread[:, 0, :]), halves_of(spread[:, 2, :]), "h%d" % t)
-            if i == CHUNKS:
+            if i == blend_step:
                 nc.vector.tensor_sub(out=c_minus_h[:], in0=c_sb[:], in1=h_sb[:])
+            if i == CHUNKS:
                 finish(0)
             if i == n_steps - 1:
                 finish(1)

@@ -21,7 +21,6 @@ H = 1024
 EPS = 1e-5
 
 K_PASS = 512
-WORDS = K_PASS // 2
 HALF = 512
 HALVES = H // HALF
 UNIT = 4
@@ -29,7 +28,6 @@ BANK_TURNS = 4
 UNIT_BANKS = 2 * UNIT // BANK_TURNS
 H_GROUPS = H // K_PASS
 CHUNKS = IN // (UNIT * K_PASS)
-LAG_CHUNKS = 2
 RUN_CHUNKS = 2
 RUNS = CHUNKS // RUN_CHUNKS
 X_BUFFERS = 6
@@ -39,26 +37,19 @@ FLOPS = 2 * ROWS * (IN + H) * H
 
 H_UNIT = ("h", 0, 0)
 
-
-def plan_steps():
-    steps = [[H_UNIT]]
-    for c in range(CHUNKS):
-        behind = [("x", 1, c - LAG_CHUNKS)] if c >= LAG_CHUNKS else []
-        steps.append([("x", 0, c)] + behind)
-    rest = [("x", 1, c) for c in range(CHUNKS - LAG_CHUNKS, CHUNKS)]
-    for first in range(0, LAG_CHUNKS, 2):
-        steps.append(rest[first : first + 2])
-    return steps
+HEAD = 0
+SPLIT_LAST_RUN = True
+U7_PIECES = 4
+SC4 = False
+TAIL = 1
 
 
 def tile_layernormgrucell_pb_k_kernel(
     tc, x, h, c, W_u_words, W_u_scales, U_u_words, U_u_scales, ln_gamma, ln_beta, out
 ):
     nc = tc.nc
-    steps = plan_steps()
+    steps = [[H_UNIT]] + [[("x", t, chunk) for t in range(ROW_TILES)] for chunk in range(CHUNKS)]
     n_steps = len(steps)
-    n_spread = 3
-    assert all(len(steps[s]) == 1 for s in range(n_spread))
 
     with ExitStack() as ctx:
         keep = ctx.enter_context(tc.tile_pool(name="keep", bufs=1))
@@ -82,8 +73,9 @@ def tile_layernormgrucell_pb_k_kernel(
         ones = keep.tile([P, P], BF16, name="ones")
         minus_half = keep.tile([P, 1], F32, name="minus_half")
         table_warm = keep.tile([P, 1], F32, name="table_warm")
-        spread_src = keep.tile([P, n_spread, H], BF16, name="spread_src")
-        spread = keep.tile([P, n_spread, H], F32, name="spread")
+        spread_src = keep.tile([P, 3, H], BF16, name="spread_src")
+        gammas = keep.tile([P, 2, H], BF16, name="gammas")
+        beta_sum = keep.tile([P, H], F32, name="beta_sum")
         hidden_term = [keep.tile([P, H], F32, name="hidden_term%d" % t) for t in range(ROW_TILES)]
         c_minus_h = keep.tile([P, ROW_TILES, H], F32, name="c_minus_h")
         result = [keep.tile([P, H], F32, name="result%d" % t) for t in range(ROW_TILES)]
@@ -108,41 +100,48 @@ def tile_layernormgrucell_pb_k_kernel(
                     raw[unit] = x_raw[:]
 
         def load_plane(plane, scales_dram):
-            for low_q in range(2):
+            if SC4:
                 for r in range(4):
                     nc.sync.dma_start(
-                        out=plane[32 * low_q + r : P : 64, :, :].bitcast(I32),
-                        in_=scales_dram[:, 4 * low_q + r : 16 : 8, :].rearrange("g q n -> q g n"),
+                        out=plane[r:P:32, :, :].bitcast(I32),
+                        in_=scales_dram[:, r:16:4, :].rearrange("g q n -> q g n"),
                     )
+            else:
+                for low_q in range(2):
+                    for r in range(4):
+                        nc.sync.dma_start(
+                            out=plane[32 * low_q + r : P : 64, :, :].bitcast(I32),
+                            in_=scales_dram[:, 4 * low_q + r : 16 : 8, :].rearrange("g q n -> q g n"),
+                        )
 
         w_words_dram = W_u_words.bitcast(I32)
         w_scales_dram = W_u_scales.bitcast(I32)
         u_words_dram = U_u_words.bitcast(I32)
         u_scales_dram = U_u_scales.bitcast(I32)
 
-        def load_scales(step):
-            for unit in steps[step]:
-                if unit == H_UNIT:
-                    load_plane(w_plane, w_scales_dram)
-                elif unit[1] == 0 and unit[2] % RUN_CHUNKS == 0:
-                    run = unit[2] // RUN_CHUNKS
-                    groups = slice(run * RUN_CHUNKS * UNIT, (run + 1) * RUN_CHUNKS * UNIT)
-                    load_plane(u_plane[run], u_scales_dram[groups])
-
-        def load_words(step):
-            for unit in steps[step]:
-                if unit == H_UNIT:
-                    nc.sync.dma_start(out=w_words[:].bitcast(I32), in_=w_words_dram.rearrange("g p b -> p g b"))
-                elif unit[1] == 0:
-                    groups = slice(unit[2] * UNIT, (unit[2] + 1) * UNIT)
-                    nc.sync.dma_start(
-                        out=u_words[unit[2]][:].bitcast(I32),
-                        in_=u_words_dram[groups].rearrange("g p b -> p g b"),
-                    )
+        def load_weights(step):
+            if step == 0:
+                load_plane(w_plane, w_scales_dram)
+                nc.sync.dma_start(out=w_words[:].bitcast(I32), in_=w_words_dram.rearrange("g p b -> p g b"))
+                return
+            chunk = step - 1
+            run, in_run = chunk // RUN_CHUNKS, chunk % RUN_CHUNKS
+            if SPLIT_LAST_RUN and run == RUNS - 1:
+                load_plane(
+                    u_plane[run][:, in_run * UNIT : (in_run + 1) * UNIT, :],
+                    u_scales_dram[chunk * UNIT : (chunk + 1) * UNIT],
+                )
+            elif in_run == 0:
+                load_plane(u_plane[run], u_scales_dram[chunk * UNIT : (chunk + RUN_CHUNKS) * UNIT])
+            piece = UNIT // U7_PIECES if chunk == CHUNKS - 1 else UNIT
+            for first in range(0, UNIT, piece):
+                nc.sync.dma_start(
+                    out=u_words[chunk][:, first : first + piece, :].bitcast(I32),
+                    in_=u_words_dram[chunk * UNIT + first : chunk * UNIT + first + piece].rearrange("g p b -> p g b"),
+                )
 
         sorted_words = {}
         turned = {}
-        spread_banks = {}
         codes = {}
         code_scales = {}
 
@@ -166,18 +165,6 @@ def tile_layernormgrucell_pb_k_kernel(
                             out=turn[:, q, :], in_=sorted_words[unit][:, operand, q % 2, :], identity=identity[:]
                         )
                     turned[unit].append(turn)
-            if step < n_spread:
-                spread_banks[step] = []
-                for half in range(HALVES):
-                    turn = turn_pool.tile([P, HALF], F32, name="turn")
-                    nc.tensor.matmul(
-                        out=turn[:],
-                        lhsT=ones[:],
-                        rhs=spread_src[:, step, half * HALF : (half + 1) * HALF],
-                        start=True,
-                        stop=True,
-                    )
-                    spread_banks[step].append(turn)
 
         def regroup_and_quantise(step):
             grouped = {}
@@ -190,11 +177,6 @@ def tile_layernormgrucell_pb_k_kernel(
                         out=as_words[:, bank * per_bank : (bank + 1) * per_bank, :, :],
                         in_=turned[unit][bank][:].rearrange("p (k u) r -> p k r u", u=2),
                     )
-            if step < n_spread:
-                for half in range(HALVES):
-                    nc.scalar.copy(
-                        out=spread[:, step, half * HALF : (half + 1) * HALF], in_=spread_banks[step][half][:]
-                    )
             for unit in steps[step]:
                 codes[unit] = step_pool.tile([P, UNIT * P], U32, name="codes", align_bytes=64)
                 code_scales[unit] = step_pool.tile([P, UNIT * P], U8, name="code_scales", align_bytes=64)
@@ -204,39 +186,54 @@ def tile_layernormgrucell_pb_k_kernel(
 
         sums = {}
 
-        def open_sums(name, t):
-            sums[(name, t)] = [
-                sum_pool.tile([P, HALF], F32, name="sum_%s%d%d" % (name, t, half), tag="sum%d%d" % (t, half))
-                for half in range(HALVES)
-            ]
+        def bank_of(name, t, half, shape, dtype):
+            return sum_pool.tile(shape, dtype, name="%s%d%d" % (name, t, half), tag="sum%d%d" % (t, half))
 
-        def multiply(step):
-            for half in range(HALVES):
-                for unit in steps[step]:
-                    for k in range(UNIT):
-                        if unit == H_UNIT:
-                            t, group, last_group = k // H_GROUPS, k % H_GROUPS, H_GROUPS - 1
-                            words, plane = w_words[:, group, :], w_plane[:, group, :]
-                        else:
-                            t, group, last_group = unit[1], unit[2] * UNIT + k, CHUNKS * UNIT - 1
-                            words = u_words[unit[2]][:, k, :]
-                            plane = u_plane[unit[2] // RUN_CHUNKS][:, group % (RUN_CHUNKS * UNIT), :]
-                        if group == 0 and half == 0:
-                            open_sums(unit[0], t)
-                        nc.tensor.matmul_mx(
-                            out=sums[(unit[0], t)][half][:],
-                            lhsT=codes[unit][:, k * P : (k + 1) * P].bitcast(FP8X4),
-                            lhsT_scale=code_scales[unit][:, k * P : (k + 1) * P],
-                            rhs=words[:, half * 2 * HALF : (half + 1) * 2 * HALF].bitcast(FP4X4),
-                            rhs_scale=plane[:, half * HALF : (half + 1) * HALF],
-                            start=(group == 0),
-                            stop=(group == last_group),
-                        )
+        def multiply(units, by_group=False):
+            if by_group:
+                order = [(half, unit, k) for unit in units for k in range(UNIT) for half in range(HALVES)]
+            else:
+                order = [(half, unit, k) for half in range(HALVES) for unit in units for k in range(UNIT)]
+            for half, unit, k in order:
+                if unit == H_UNIT:
+                    t, group, last_group = k // H_GROUPS, k % H_GROUPS, H_GROUPS - 1
+                    words, plane = w_words[:, group, :], w_plane[:, group, :]
+                else:
+                    t, group, last_group = unit[1], unit[2] * UNIT + k, CHUNKS * UNIT - 1
+                    words = u_words[unit[2]][:, k, :]
+                    plane = u_plane[unit[2] // RUN_CHUNKS][:, group % (RUN_CHUNKS * UNIT), :]
+                if group == 0:
+                    sums[(unit[0], t, half)] = bank_of("sum_" + unit[0], t, half, [P, HALF], F32)
+                nc.tensor.matmul_mx(
+                    out=sums[(unit[0], t, half)][:],
+                    lhsT=codes[unit][:, k * P : (k + 1) * P].bitcast(FP8X4),
+                    lhsT_scale=code_scales[unit][:, k * P : (k + 1) * P],
+                    rhs=words[:, half * 2 * HALF : (half + 1) * 2 * HALF].bitcast(FP4X4),
+                    rhs_scale=plane[:, half * HALF : (half + 1) * HALF],
+                    start=(group == 0),
+                    stop=(group == last_group),
+                )
 
         def halves_of(tile_ap):
             return [tile_ap[:, half * HALF : (half + 1) * HALF] for half in range(HALVES)]
 
-        def norm_scale_add(dst, src, gamma, addend, name):
+        def spread_constants():
+            for row in range(2):
+                bank = bank_of("spread", 0, row, [P, H], BF16)
+                for half in range(HALVES):
+                    nc.tensor.matmul(
+                        out=halves_of(bank)[half], lhsT=ones[:], rhs=halves_of(spread_src[:, row, :])[half],
+                        start=True, stop=True,
+                    )
+                nc.scalar.copy(out=gammas[:, row, :], in_=bank[:])
+            for half in range(HALVES):
+                bank = bank_of("spread", 1, half, [P, HALF], F32)
+                nc.tensor.matmul(
+                    out=bank[:], lhsT=ones[:], rhs=halves_of(spread_src[:, 2, :])[half], start=True, stop=True
+                )
+                nc.scalar.copy(out=halves_of(beta_sum)[half], in_=bank[:])
+
+        def statistics(src, name):
             stats = keep.tile([P, HALVES, 6], F32, name="stats_" + name)
             mean_var = keep.tile([P, 2], F32, name="mean_var_" + name)
             var_eps = keep.tile([P, 1], F32, name="var_eps_" + name)
@@ -246,25 +243,34 @@ def tile_layernormgrucell_pb_k_kernel(
             nc.vector.bn_aggr(out=mean_var[:], in_=stats[:].rearrange("p a s -> p (a s)"))
             nc.vector.tensor_scalar_add(out=var_eps[:], in0=mean_var[:, 1:2], scalar1=EPS)
             nc.gpsimd.tensor_tensor(out=inv_std[:], in0=var_eps[:], in1=minus_half[:], op=ALU.pow)
+            return mean_var[:, 0:1], inv_std[:]
+
+        def scale_add(dst, src, mean, inv_std, gamma, addend):
             for half in range(HALVES):
                 nc.vector.scalar_tensor_tensor(
-                    out=dst[half], in0=src[half], scalar=mean_var[:, 0:1], in1=gamma[half],
-                    op0=ALU.subtract, op1=ALU.mult,
+                    out=dst[half], in0=src[half], scalar=mean, in1=gamma[half], op0=ALU.subtract, op1=ALU.mult
                 )
             for half in range(HALVES):
                 nc.vector.scalar_tensor_tensor(
-                    out=dst[half], in0=dst[half], scalar=inv_std[:], in1=addend[half],
-                    op0=ALU.mult, op1=ALU.add,
+                    out=dst[half], in0=dst[half], scalar=inv_std, in1=addend[half], op0=ALU.mult, op1=ALU.add
                 )
 
-        def finish(t):
+        x_stats = {}
+
+        def x_sums(t):
+            return [sums[("x", t, half)][:] for half in range(HALVES)]
+
+        def finish_statistics(t):
+            x_stats[t] = statistics(x_sums(t), "x%d" % t)
+
+        def finish_gate(t):
             res = halves_of(result[t])
-            norm_scale_add(
-                res, [s[:] for s in sums[("x", t)]], halves_of(spread[:, 1, :]), halves_of(hidden_term[t]),
-                "x%d" % t,
-            )
+            scale_add(res, x_sums(t), x_stats[t][0], x_stats[t][1], halves_of(gammas[:, 1, :]), halves_of(hidden_term[t]))
             for half in range(HALVES):
                 nc.scalar.activation(out=res[half], in_=res[half], func=ACT.Sigmoid)
+
+        def finish_blend(t):
+            res = halves_of(result[t])
             for half in range(HALVES):
                 nc.vector.tensor_mul(out=res[half], in0=res[half], in1=halves_of(c_minus_h[:, t, :])[half])
             for half in range(HALVES):
@@ -282,46 +288,65 @@ def tile_layernormgrucell_pb_k_kernel(
         nc.scalar.activation(out=table_warm[:], in_=minus_half[:], func=ACT.Sigmoid)
 
         load_activations(0)
-        load_activations(1)
-        nc.sync.dma_start(out=spread_src[0:1, 0:2, :], in_=ln_gamma.unsqueeze(0))
-        nc.sync.dma_start(out=spread_src[0:2, 2, :], in_=ln_beta)
-        load_scales(0)
-        load_scales(1)
-        load_words(0)
-        load_activations(2)
-        load_words(1)
+        if HEAD == 0:
+            load_activations(1)
+            nc.sync.dma_start(out=spread_src[0:1, 0:2, :], in_=ln_gamma.unsqueeze(0))
+            nc.sync.dma_start(out=spread_src[0:2, 2, :], in_=ln_beta)
+            load_weights(0)
+            load_activations(2)
+            load_weights(1)
+        else:
+            nc.sync.dma_start(out=spread_src[0:1, 0:2, :], in_=ln_gamma.unsqueeze(0))
+            nc.sync.dma_start(out=spread_src[0:2, 2, :], in_=ln_beta)
+            load_weights(0)
+            load_activations(1)
+            load_weights(1)
+            load_activations(2)
         sort_words(0)
 
-        first_norm_step = n_spread - 1
+        first_norm_step = 1
         blend_step = n_steps // 2
-        for i in range(-1, n_steps):
+        for i in range(-1, n_steps - 1):
             if i + 4 < n_steps:
                 load_activations(i + 4)
             if i + 3 < n_steps:
-                load_scales(i + 3)
-                load_words(i + 3)
+                load_weights(i + 3)
             if i + 3 == blend_step:
                 nc.sync.dma_start(out=c_sb[:], in_=c.rearrange("(t p) k -> p t k", p=P))
-            if i + 1 < n_steps:
-                transpose(i + 1)
-                regroup_and_quantise(i + 1)
+            transpose(i + 1)
+            regroup_and_quantise(i + 1)
+            if i == -1:
+                spread_constants()
             if i + 2 < n_steps:
                 sort_words(i + 2)
             if 1 <= i + 2 < RUNS:
                 zero_plane(u_plane[i + 2])
-            if i >= 0:
-                multiply(i)
+            if 0 <= i < n_steps - 2:
+                multiply(steps[i])
             if i == 0:
                 for half in range(HALVES):
                     for t in range(ROW_TILES):
-                        nc.scalar.copy(out=halves_of(hidden_term[t])[half], in_=sums[("h", t)][half][:])
+                        nc.scalar.copy(out=halves_of(hidden_term[t])[half], in_=sums[("h", t, half)][:])
             if 0 <= i - first_norm_step < ROW_TILES:
                 t = i - first_norm_step
                 term = halves_of(hidden_term[t])
-                norm_scale_add(term, term, halves_of(spread[:, 0, :]), halves_of(spread[:, 2, :]), "h%d" % t)
+                mean, inv_std = statistics(term, "h%d" % t)
+                scale_add(term, term, mean, inv_std, halves_of(gammas[:, 0, :]), halves_of(beta_sum))
             if i == blend_step:
                 nc.vector.tensor_sub(out=c_minus_h[:], in0=c_sb[:], in1=h_sb[:])
-            if i == CHUNKS:
-                finish(0)
-            if i == n_steps - 1:
-                finish(1)
+
+        last = [steps[n_steps - 2], steps[n_steps - 1]]
+        if TAIL == 0:
+            multiply(last[0])
+            multiply(last[1])
+        else:
+            multiply([last[0][0]])
+            multiply([last[1][0]], by_group=True)
+        finish_statistics(0)
+        if TAIL == 1:
+            multiply([last[0][1], last[1][1]])
+        finish_gate(0)
+        finish_statistics(1)
+        finish_gate(1)
+        finish_blend(0)
+        finish_blend(1)

@@ -38,10 +38,17 @@ FLOPS = 2 * ROWS * (IN + H) * H
 H_UNIT = ("h", 0, 0)
 
 HEAD = 0
+U0_PIECES = 1
 SPLIT_LAST_RUN = True
 U7_PIECES = 4
 SC4 = False
 TAIL = 1
+C_LAST = True
+REGROUP = 2
+PE_ADD0 = False
+SEQ = False
+ADD0_GPSIMD = False
+CODE_BUFFERS = 2 * (REGROUP + 1)
 
 
 def tile_layernormgrucell_pb_k_kernel(
@@ -57,6 +64,7 @@ def tile_layernormgrucell_pb_k_kernel(
         step_pool = ctx.enter_context(tc.tile_pool(name="step_pool", bufs=STEP_BUFFERS))
         sum_pool = ctx.enter_context(tc.psum_pool(name="sum_pool", bufs=1))
         turn_pool = ctx.enter_context(tc.psum_pool(name="turn_pool", bufs=2 * UNIT_BANKS))
+        code_pool = ctx.enter_context(tc.tile_pool(name="code_pool", bufs=CODE_BUFFERS))
         ctx.enter_context(tc.manual_schedule())
 
         h_sb = keep.tile([P, ROW_TILES, H], BF16, name="h_sb")
@@ -77,7 +85,9 @@ def tile_layernormgrucell_pb_k_kernel(
         gammas = keep.tile([P, 2, H], BF16, name="gammas")
         beta_sum = keep.tile([P, H], F32, name="beta_sum")
         hidden_term = [keep.tile([P, H], F32, name="hidden_term%d" % t) for t in range(ROW_TILES)]
-        c_minus_h = keep.tile([P, ROW_TILES, H], F32, name="c_minus_h")
+        c_minus_h_sb = None if C_LAST else keep.tile([P, ROW_TILES, H], F32, name="c_minus_h_sb")
+        plus_one = keep.tile([P, P], BF16, name="plus_one")
+        minus_one = keep.tile([P, P], BF16, name="minus_one")
         result = [keep.tile([P, H], F32, name="result%d" % t) for t in range(ROW_TILES)]
 
         def zero_plane(plane):
@@ -126,14 +136,14 @@ def tile_layernormgrucell_pb_k_kernel(
                 return
             chunk = step - 1
             run, in_run = chunk // RUN_CHUNKS, chunk % RUN_CHUNKS
-            if SPLIT_LAST_RUN and run == RUNS - 1:
+            if (SPLIT_LAST_RUN and run == RUNS - 1) or (HEAD == 2 and run == 0):
                 load_plane(
                     u_plane[run][:, in_run * UNIT : (in_run + 1) * UNIT, :],
                     u_scales_dram[chunk * UNIT : (chunk + 1) * UNIT],
                 )
             elif in_run == 0:
                 load_plane(u_plane[run], u_scales_dram[chunk * UNIT : (chunk + RUN_CHUNKS) * UNIT])
-            piece = UNIT // U7_PIECES if chunk == CHUNKS - 1 else UNIT
+            piece = UNIT // U7_PIECES if chunk == CHUNKS - 1 else (UNIT // U0_PIECES if chunk == 0 else UNIT)
             for first in range(0, UNIT, piece):
                 nc.sync.dma_start(
                     out=u_words[chunk][:, first : first + piece, :].bitcast(I32),
@@ -178,8 +188,8 @@ def tile_layernormgrucell_pb_k_kernel(
                         in_=turned[unit][bank][:].rearrange("p (k u) r -> p k r u", u=2),
                     )
             for unit in steps[step]:
-                codes[unit] = step_pool.tile([P, UNIT * P], U32, name="codes", align_bytes=64)
-                code_scales[unit] = step_pool.tile([P, UNIT * P], U8, name="code_scales", align_bytes=64)
+                codes[unit] = code_pool.tile([P, UNIT * P], U32, name="codes", align_bytes=64)
+                code_scales[unit] = code_pool.tile([P, UNIT * P], U8, name="code_scales", align_bytes=64)
                 nc.vector.quantize_mx(
                     out=codes[unit][:].bitcast(FP8X4), scales=code_scales[unit][:], in_=grouped[unit][:]
                 )
@@ -189,11 +199,11 @@ def tile_layernormgrucell_pb_k_kernel(
         def bank_of(name, t, half, shape, dtype):
             return sum_pool.tile(shape, dtype, name="%s%d%d" % (name, t, half), tag="sum%d%d" % (t, half))
 
-        def multiply(units, by_group=False):
+        def multiply(units, by_group=False, halves=(0, 1)):
             if by_group:
                 order = [(half, unit, k) for unit in units for k in range(UNIT) for half in range(HALVES)]
             else:
-                order = [(half, unit, k) for half in range(HALVES) for unit in units for k in range(UNIT)]
+                order = [(half, unit, k) for half in halves for unit in units for k in range(UNIT)]
             for half, unit, k in order:
                 if unit == H_UNIT:
                     t, group, last_group = k // H_GROUPS, k % H_GROUPS, H_GROUPS - 1
@@ -269,15 +279,45 @@ def tile_layernormgrucell_pb_k_kernel(
             for half in range(HALVES):
                 nc.scalar.activation(out=res[half], in_=res[half], func=ACT.Sigmoid)
 
-        def finish_blend(t):
+        c_minus_h = {}
+
+        def open_c_minus_h(t):
+            for half in range(HALVES):
+                if C_LAST:
+                    bank = turn_pool.tile([P, HALF], F32, name="turn")
+                    nc.tensor.matmul(out=bank[:], lhsT=minus_one[:], rhs=halves_of(h_sb[:, t, :])[half], start=True, stop=False)
+                    c_minus_h[(t, half)] = bank[:]
+                else:
+                    c_minus_h[(t, half)] = halves_of(c_minus_h_sb[:, t, :])[half]
+
+        def close_c_minus_h(t):
+            for half in range(HALVES):
+                if C_LAST:
+                    nc.tensor.matmul(
+                        out=c_minus_h[(t, half)], lhsT=plus_one[:], rhs=halves_of(c_sb[:, t, :])[half], start=False, stop=True
+                    )
+
+        def store(t, half, src):
+            nc.sync.dma_start(out=out[t * P : (t + 1) * P, half * HALF : (half + 1) * HALF], in_=src)
+
+        def finish_blend(t, add_on_tensor):
             res = halves_of(result[t])
             for half in range(HALVES):
-                nc.vector.tensor_mul(out=res[half], in0=res[half], in1=halves_of(c_minus_h[:, t, :])[half])
+                nc.vector.tensor_mul(out=res[half], in0=res[half], in1=c_minus_h[(t, half)])
             for half in range(HALVES):
-                nc.vector.tensor_add(out=res[half], in0=res[half], in1=halves_of(h_sb[:, t, :])[half])
-                nc.sync.dma_start(
-                    out=out[t * P : (t + 1) * P, half * HALF : (half + 1) * HALF], in_=res[half]
-                )
+                if add_on_tensor:
+                    bank = bank_of("blend", t, half, [P, HALF], F32)
+                    nc.tensor.matmul(out=bank[:], lhsT=plus_one[:], rhs=halves_of(h_sb[:, t, :])[half], start=True, stop=False)
+                    nc.tensor.matmul(out=bank[:], lhsT=identity[:], rhs=res[half], start=False, stop=True)
+                    blended = keep.tile([P, HALF], F32, name="blended%d%d" % (t, half))
+                    nc.scalar.copy(out=blended[:], in_=bank[:])
+                    store(t, half, blended[:])
+                elif ADD0_GPSIMD and t == 0:
+                    nc.gpsimd.tensor_tensor(out=res[half], in0=res[half], in1=halves_of(h_sb[:, t, :])[half], op=ALU.add)
+                    store(t, half, res[half])
+                else:
+                    nc.vector.tensor_add(out=res[half], in0=res[half], in1=halves_of(h_sb[:, t, :])[half])
+                    store(t, half, res[half])
 
         zero_plane(w_plane)
         zero_plane(u_plane[0])
@@ -285,6 +325,8 @@ def tile_layernormgrucell_pb_k_kernel(
         nc.gpsimd.memset(spread_src[:].bitcast(F32), 0.0)
         make_identity(nc, identity[:])
         nc.gpsimd.memset(ones[:], 1.0)
+        nc.gpsimd.tensor_copy(out=plus_one[:], in_=identity[:])
+        nc.gpsimd.tensor_scalar(out=minus_one[:], in0=identity[:], scalar1=-1.0, scalar2=0.0, op0=ALU.mult, op1=ALU.add)
         nc.scalar.activation(out=table_warm[:], in_=minus_half[:], func=ACT.Sigmoid)
 
         load_activations(0)
@@ -311,8 +353,10 @@ def tile_layernormgrucell_pb_k_kernel(
                 load_activations(i + 4)
             if i + 3 < n_steps:
                 load_weights(i + 3)
-            if i + 3 == blend_step:
+            if i + 3 == (n_steps - 1 if C_LAST else blend_step):
                 nc.sync.dma_start(out=c_sb[:], in_=c.rearrange("(t p) k -> p t k", p=P))
+            if HEAD == 2 and i == 1:
+                multiply(steps[i], by_group=(U0_PIECES > 1))
             transpose(i + 1)
             regroup_and_quantise(i + 1)
             if i == -1:
@@ -321,8 +365,12 @@ def tile_layernormgrucell_pb_k_kernel(
                 sort_words(i + 2)
             if 1 <= i + 2 < RUNS:
                 zero_plane(u_plane[i + 2])
-            if 0 <= i < n_steps - 2:
+            if HEAD == 2 and i == 1:
+                pass
+            elif 0 <= i < n_steps - REGROUP:
                 multiply(steps[i])
+            elif i >= 0:
+                multiply(steps[i][0:1])
             if i == 0:
                 for half in range(HALVES):
                     for t in range(ROW_TILES):
@@ -332,21 +380,23 @@ def tile_layernormgrucell_pb_k_kernel(
                 term = halves_of(hidden_term[t])
                 mean, inv_std = statistics(term, "h%d" % t)
                 scale_add(term, term, mean, inv_std, halves_of(gammas[:, 0, :]), halves_of(beta_sum))
-            if i == blend_step:
-                nc.vector.tensor_sub(out=c_minus_h[:], in0=c_sb[:], in1=h_sb[:])
+            if i == blend_step and not C_LAST:
+                nc.vector.tensor_sub(out=c_minus_h_sb[:], in0=c_sb[:], in1=h_sb[:])
 
-        last = [steps[n_steps - 2], steps[n_steps - 1]]
-        if TAIL == 0:
-            multiply(last[0])
-            multiply(last[1])
-        else:
-            multiply([last[0][0]])
-            multiply([last[1][0]], by_group=True)
+        multiply(steps[n_steps - 1][0:1], by_group=True)
         finish_statistics(0)
-        if TAIL == 1:
-            multiply([last[0][1], last[1][1]])
+        owed = [steps[s][1] for s in range(n_steps - REGROUP, n_steps)]
+        multiply(owed)
+        for t in range(ROW_TILES):
+            open_c_minus_h(t)
+            close_c_minus_h(t)
         finish_gate(0)
-        finish_statistics(1)
-        finish_gate(1)
-        finish_blend(0)
-        finish_blend(1)
+        if SEQ:
+            finish_blend(0, PE_ADD0)
+            finish_statistics(1)
+            finish_gate(1)
+        else:
+            finish_statistics(1)
+            finish_gate(1)
+            finish_blend(0, PE_ADD0)
+        finish_blend(1, False)

@@ -47,6 +47,7 @@ C_LAST = True
 REGROUP = 2
 PE_ADD0 = False
 SEQ = False
+VTAIL = 1
 ADD0_GPSIMD = False
 CODE_BUFFERS = 2 * (REGROUP + 1)
 
@@ -245,11 +246,14 @@ def tile_layernormgrucell_pb_k_kernel(
 
         def statistics(src, name):
             stats = keep.tile([P, HALVES, 6], F32, name="stats_" + name)
+            for half in range(HALVES):
+                nc.vector.bn_stats(out=stats[:, half, :], in_=src[half])
+            return aggregate(stats, name)
+
+        def aggregate(stats, name):
             mean_var = keep.tile([P, 2], F32, name="mean_var_" + name)
             var_eps = keep.tile([P, 1], F32, name="var_eps_" + name)
             inv_std = keep.tile([P, 1], F32, name="inv_std_" + name)
-            for half in range(HALVES):
-                nc.vector.bn_stats(out=stats[:, half, :], in_=src[half])
             nc.vector.bn_aggr(out=mean_var[:], in_=stats[:].rearrange("p a s -> p (a s)"))
             nc.vector.tensor_scalar_add(out=var_eps[:], in0=mean_var[:, 1:2], scalar1=EPS)
             nc.gpsimd.tensor_tensor(out=inv_std[:], in0=var_eps[:], in1=minus_half[:], op=ALU.pow)
@@ -274,10 +278,37 @@ def tile_layernormgrucell_pb_k_kernel(
             x_stats[t] = statistics(x_sums(t), "x%d" % t)
 
         def finish_gate(t):
+            finish_centre(t)
+            finish_sigmoid(t)
+
+        def finish_centre(t):
             res = halves_of(result[t])
-            scale_add(res, x_sums(t), x_stats[t][0], x_stats[t][1], halves_of(gammas[:, 1, :]), halves_of(hidden_term[t]))
+            for half in range(HALVES):
+                nc.vector.scalar_tensor_tensor(
+                    out=res[half], in0=x_sums(t)[half], scalar=x_stats[t][0], in1=halves_of(gammas[:, 1, :])[half],
+                    op0=ALU.subtract, op1=ALU.mult,
+                )
+
+        def finish_sigmoid(t):
+            res = halves_of(result[t])
+            for half in range(HALVES):
+                nc.vector.scalar_tensor_tensor(
+                    out=res[half], in0=res[half], scalar=x_stats[t][1], in1=halves_of(hidden_term[t])[half],
+                    op0=ALU.mult, op1=ALU.add,
+                )
             for half in range(HALVES):
                 nc.scalar.activation(out=res[half], in_=res[half], func=ACT.Sigmoid)
+
+        def finish_multiply(t):
+            res = halves_of(result[t])
+            for half in range(HALVES):
+                nc.vector.tensor_mul(out=res[half], in0=res[half], in1=c_minus_h[(t, half)])
+
+        def finish_add(t):
+            res = halves_of(result[t])
+            for half in range(HALVES):
+                nc.vector.tensor_add(out=res[half], in0=res[half], in1=halves_of(h_sb[:, t, :])[half])
+                store(t, half, res[half])
 
         c_minus_h = {}
 
@@ -390,13 +421,22 @@ def tile_layernormgrucell_pb_k_kernel(
         for t in range(ROW_TILES):
             open_c_minus_h(t)
             close_c_minus_h(t)
-        finish_gate(0)
-        if SEQ:
-            finish_blend(0, PE_ADD0)
+        if VTAIL == 0:
+            finish_gate(0)
             finish_statistics(1)
             finish_gate(1)
+            finish_blend(0, False)
+            finish_blend(1, False)
         else:
-            finish_statistics(1)
-            finish_gate(1)
-            finish_blend(0, PE_ADD0)
-        finish_blend(1, False)
+            stats1 = keep.tile([P, HALVES, 6], F32, name="stats_x1")
+            finish_centre(0)
+            nc.vector.bn_stats(out=stats1[:, 0, :], in_=x_sums(1)[0])
+            finish_sigmoid(0)
+            nc.vector.bn_stats(out=stats1[:, 1, :], in_=x_sums(1)[1])
+            x_stats[1] = aggregate(stats1, "x1")
+            finish_centre(1)
+            finish_multiply(0)
+            finish_sigmoid(1)
+            finish_add(0)
+            finish_multiply(1)
+            finish_add(1)

from contextlib import ExitStack

import concourse.mybir as mybir
from concourse.masks import make_identity

F32 = mybir.dt.float32
BF16 = mybir.dt.bfloat16
U8 = mybir.dt.uint8
U32 = mybir.dt.uint32
I32 = mybir.dt.int32
FP8X4 = mybir.dt.float8_e4m3fn_x4
FP4X4 = mybir.dt.float4_e2m1fn_x4
ALU = mybir.AluOpType
ACT = mybir.ActivationFunctionType

P = 128
ROWS = 256
ROW_TILES = ROWS // P
IN = 16384
H = 1024
EPS = 1e-5

K_PASS = 512
HALF = 512
HALVES = H // HALF
UNIT = 4
BANK_TURNS = 4
UNIT_BANKS = 2 * UNIT // BANK_TURNS
H_GROUPS = H // K_PASS
CHUNKS = IN // (UNIT * K_PASS)
RUN_CHUNKS = 2
RUNS = CHUNKS // RUN_CHUNKS
X_BUFFERS = 6
STEP_BUFFERS = 4

FLOPS = 2 * ROWS * (IN + H) * H

H_UNIT = ("h", 0, 0)

HEAD = 0
U0_PIECES = 1
SPLIT_LAST_RUN = True
U7_PIECES = 4
SC4 = False
TAIL = 1
C_LAST = True
REGROUP = 2
PE_ADD0 = False
SEQ = False
VTAIL = 1
ADD0_GPSIMD = False
CODE_BUFFERS = 2 * (REGROUP + 1)


def tile_layernormgrucell_pb_k_kernel(
    tc, x, h, c, W_u_words, W_u_scales, U_u_words, U_u_scales, ln_gamma, ln_beta, out
):
    nc = tc.nc
    steps = [[H_UNIT]] + [[("x", t, chunk) for t in range(ROW_TILES)] for chunk in range(CHUNKS)]
    n_steps = len(steps)

    with ExitStack() as ctx:
        keep = ctx.enter_context(tc.tile_pool(name="keep", bufs=1))
        x_pool = ctx.enter_context(tc.tile_pool(name="x_pool", bufs=X_BUFFERS))
        step_pool = ctx.enter_context(tc.tile_pool(name="step_pool", bufs=STEP_BUFFERS))
        sum_pool = ctx.enter_context(tc.psum_pool(name="sum_pool", bufs=1))
        turn_pool = ctx.enter_context(tc.psum_pool(name="turn_pool", bufs=2 * UNIT_BANKS))
        code_pool = ctx.enter_context(tc.tile_pool(name="code_pool", bufs=CODE_BUFFERS))
        ctx.enter_context(tc.manual_schedule())

        h_sb = keep.tile([P, ROW_TILES, H], BF16, name="h_sb")
        c_sb = keep.tile([P, ROW_TILES, H], BF16, name="c_sb")
        w_words = keep.tile([P, H_GROUPS, 2 * H], U8, name="w_words", align_bytes=64)
        w_plane = keep.tile([P, H_GROUPS, H], U8, name="w_plane", align_bytes=64)
        u_words = [
            keep.tile([P, UNIT, 2 * H], U8, name="u_words%d" % k, align_bytes=64) for k in range(CHUNKS)
        ]
        u_plane = [
            keep.tile([P, RUN_CHUNKS * UNIT, H], U8, name="u_plane%d" % k, align_bytes=64) for k in range(RUNS)
        ]
        identity = keep.tile([P, P], F32, name="identity")
        ones = keep.tile([P, P], BF16, name="ones")
        minus_half = keep.tile([P, 1], F32, name="minus_half")
        table_warm = keep.tile([P, 1], F32, name="table_warm")
        spread_src = keep.tile([P, 3, H], BF16, name="spread_src")
        gammas = keep.tile([P, 2, H], BF16, name="gammas")
        beta_sum = keep.tile([P, H], F32, name="beta_sum")
        hidden_term = [keep.tile([P, H], F32, name="hidden_term%d" % t) for t in range(ROW_TILES)]
        c_minus_h_sb = None if C_LAST else keep.tile([P, ROW_TILES, H], F32, name="c_minus_h_sb")
        plus_one = keep.tile([P, P], BF16, name="plus_one")
        minus_one = keep.tile([P, P], BF16, name="minus_one")
        result = [keep.tile([P, H], F32, name="result%d" % t) for t in range(ROW_TILES)]

        def zero_plane(plane):
            nc.vector.memset(plane[:].bitcast(I32), 0)

        raw = {}

        def load_activations(step):
            for unit in steps[step]:
                if unit == H_UNIT:
                    nc.sync.dma_start(out=h_sb[:], in_=h.rearrange("(t p) k -> p t k", p=P))
                    raw[unit] = h_sb[:].rearrange("p t k -> p (t k)")
                else:
                    t, chunk = unit[1], unit[2]
                    x_raw = x_pool.tile([P, UNIT * K_PASS], BF16, name="x_raw")
                    nc.sync.dma_start(
                        out=x_raw[:],
                        in_=x[t * P : (t + 1) * P, chunk * UNIT * K_PASS : (chunk + 1) * UNIT * K_PASS],
                    )
                    raw[unit] = x_raw[:]

        def load_plane(plane, scales_dram):
            if SC4:
                for r in range(4):
                    nc.sync.dma_start(
                        out=plane[r:P:32, :, :].bitcast(I32),
                        in_=scales_dram[:, r:16:4, :].rearrange("g q n -> q g n"),
                    )
            else:
                for low_q in range(2):
                    for r in range(4):
                        nc.sync.dma_start(
                            out=plane[32 * low_q + r : P : 64, :, :].bitcast(I32),
                            in_=scales_dram[:, 4 * low_q + r : 16 : 8, :].rearrange("g q n -> q g n"),
                        )

        w_words_dram = W_u_words.bitcast(I32)
        w_scales_dram = W_u_scales.bitcast(I32)
        u_words_dram = U_u_words.bitcast(I32)
        u_scales_dram = U_u_scales.bitcast(I32)

        def load_weights(step):
            if step == 0:
                load_plane(w_plane, w_scales_dram)
                nc.sync.dma_start(out=w_words[:].bitcast(I32), in_=w_words_dram.rearrange("g p b -> p g b"))
                return
            chunk = step - 1
            run, in_run = chunk // RUN_CHUNKS, chunk % RUN_CHUNKS
            if (SPLIT_LAST_RUN and run == RUNS - 1) or (HEAD == 2 and run == 0):
                load_plane(
                    u_plane[run][:, in_run * UNIT : (in_run + 1) * UNIT, :],
                    u_scales_dram[chunk * UNIT : (chunk + 1) * UNIT],
                )
            elif in_run == 0:
                load_plane(u_plane[run], u_scales_dram[chunk * UNIT : (chunk + RUN_CHUNKS) * UNIT])
            piece = UNIT // U7_PIECES if chunk == CHUNKS - 1 else (UNIT // U0_PIECES if chunk == 0 else UNIT)
            for first in range(0, UNIT, piece):
                nc.sync.dma_start(
                    out=u_words[chunk][:, first : first + piece, :].bitcast(I32),
                    in_=u_words_dram[chunk * UNIT + first : chunk * UNIT + first + piece].rearrange("g p b -> p g b"),
                )

        sorted_words = {}
        turned = {}
        codes = {}
        code_scales = {}

        def sort_words(step):
            for unit in steps[step]:
                by_parity = step_pool.tile([P, UNIT, 2, P], F32, name="by_parity")
                nc.vector.tensor_copy(
                    out=by_parity[:],
                    in_=raw[unit].bitcast(F32).rearrange("p (k w u) -> p k u w", k=UNIT, u=2),
                )
                sorted_words[unit] = by_parity

        def transpose(step):
            for unit in steps[step]:
                turned[unit] = []
                for bank in range(UNIT_BANKS):
                    turn = turn_pool.tile([P, BANK_TURNS, P], F32, name="turn")
                    for q in range(BANK_TURNS):
                        operand = (bank * BANK_TURNS + q) // 2
                        nc.tensor.transpose(
                            out=turn[:, q, :], in_=sorted_words[unit][:, operand, q % 2, :], identity=identity[:]
                        )
                    turned[unit].append(turn)

        def regroup_and_quantise(step):
            grouped = {}
            for unit in steps[step]:
                grouped[unit] = step_pool.tile([P, UNIT * K_PASS], BF16, name="grouped", align_bytes=64)
                as_words = grouped[unit][:].bitcast(F32).rearrange("p (k r u) -> p k r u", k=UNIT, u=2)
                per_bank = BANK_TURNS // 2
                for bank in range(UNIT_BANKS):
                    nc.scalar.copy(
                        out=as_words[:, bank * per_bank : (bank + 1) * per_bank, :, :],
                        in_=turned[unit][bank][:].rearrange("p (k u) r -> p k r u", u=2),
                    )
            for unit in steps[step]:
                codes[unit] = code_pool.tile([P, UNIT * P], U32, name="codes", align_bytes=64)
                code_scales[unit] = code_pool.tile([P, UNIT * P], U8, name="code_scales", align_bytes=64)
                nc.vector.quantize_mx(
                    out=codes[unit][:].bitcast(FP8X4), scales=code_scales[unit][:], in_=grouped[unit][:]
                )

        sums = {}

        def bank_of(name, t, half, shape, dtype):
            return sum_pool.tile(shape, dtype, name="%s%d%d" % (name, t, half), tag="sum%d%d" % (t, half))

        def multiply(units, by_group=False, halves=(0, 1)):
            if by_group:
                order = [(half, unit, k) for unit in units for k in range(UNIT) for half in range(HALVES)]
            else:
                order = [(half, unit, k) for half in halves for unit in units for k in range(UNIT)]
            for half, unit, k in order:
                if unit == H_UNIT:
                    t, group, last_group = k // H_GROUPS, k % H_GROUPS, H_GROUPS - 1
                    words, plane = w_words[:, group, :], w_plane[:, group, :]
                else:
                    t, group, last_group = unit[1], unit[2] * UNIT + k, CHUNKS * UNIT - 1
                    words = u_words[unit[2]][:, k, :]
                    plane = u_plane[unit[2] // RUN_CHUNKS][:, group % (RUN_CHUNKS * UNIT), :]
                if group == 0:
                    sums[(unit[0], t, half)] = bank_of("sum_" + unit[0], t, half, [P, HALF], F32)
                nc.tensor.matmul_mx(
                    out=sums[(unit[0], t, half)][:],
                    lhsT=codes[unit][:, k * P : (k + 1) * P].bitcast(FP8X4),
                    lhsT_scale=code_scales[unit][:, k * P : (k + 1) * P],
                    rhs=words[:, half * 2 * HALF : (half + 1) * 2 * HALF].bitcast(FP4X4),
                    rhs_scale=plane[:, half * HALF : (half + 1) * HALF],
                    start=(group == 0),
                    stop=(group == last_group),
                )

        def halves_of(tile_ap):
            return [tile_ap[:, half * HALF : (half + 1) * HALF] for half in range(HALVES)]

        def spread_constants():
            for row in range(2):
                bank = bank_of("spread", 0, row, [P, H], BF16)
                for half in range(HALVES):
                    nc.tensor.matmul(
                        out=halves_of(bank)[half], lhsT=ones[:], rhs=halves_of(spread_src[:, row, :])[half],
                        start=True, stop=True,
                    )
                nc.scalar.copy(out=gammas[:, row, :], in_=bank[:])
            for half in range(HALVES):
                bank = bank_of("spread", 1, half, [P, HALF], F32)
                nc.tensor.matmul(
                    out=bank[:], lhsT=ones[:], rhs=halves_of(spread_src[:, 2, :])[half], start=True, stop=True
                )
                nc.scalar.copy(out=halves_of(beta_sum)[half], in_=bank[:])

        def statistics(src, name):
            stats = keep.tile([P, HALVES, 6], F32, name="stats_" + name)
            for half in range(HALVES):
                nc.vector.bn_stats(out=stats[:, half, :], in_=src[half])
            return aggregate(stats, name)

        def aggregate(stats, name):
            mean_var = keep.tile([P, 2], F32, name="mean_var_" + name)
            var_eps = keep.tile([P, 1], F32, name="var_eps_" + name)
            inv_std = keep.tile([P, 1], F32, name="inv_std_" + name)
            nc.vector.bn_aggr(out=mean_var[:], in_=stats[:].rearrange("p a s -> p (a s)"))
            nc.vector.tensor_scalar_add(out=var_eps[:], in0=mean_var[:, 1:2], scalar1=EPS)
            nc.gpsimd.tensor_tensor(out=inv_std[:], in0=var_eps[:], in1=minus_half[:], op=ALU.pow)
            return mean_var[:, 0:1], inv_std[:]

        def scale_add(dst, src, mean, inv_std, gamma, addend):
            for half in range(HALVES):
                nc.vector.scalar_tensor_tensor(
                    out=dst[half], in0=src[half], scalar=mean, in1=gamma[half], op0=ALU.subtract, op1=ALU.mult
                )
            for half in range(HALVES):
                nc.vector.scalar_tensor_tensor(
                    out=dst[half], in0=dst[half], scalar=inv_std, in1=addend[half], op0=ALU.mult, op1=ALU.add
                )

        x_stats = {}

        def x_sums(t):
            return [sums[("x", t, half)][:] for half in range(HALVES)]

        def finish_statistics(t):
            x_stats[t] = statistics(x_sums(t), "x%d" % t)

        def finish_gate(t):
            finish_centre(t)
            finish_sigmoid(t)

        def finish_centre(t):
            res = halves_of(result[t])
            for half in range(HALVES):
                nc.vector.scalar_tensor_tensor(
                    out=res[half], in0=x_sums(t)[half], scalar=x_stats[t][0], in1=halves_of(gammas[:, 1, :])[half],
                    op0=ALU.subtract, op1=ALU.mult,
                )

        def finish_sigmoid(t):
            res = halves_of(result[t])
            for half in range(HALVES):
                nc.vector.scalar_tensor_tensor(
                    out=res[half], in0=res[half], scalar=x_stats[t][1], in1=halves_of(hidden_term[t])[half],
                    op0=ALU.mult, op1=ALU.add,
                )
            for half in range(HALVES):
                nc.scalar.activation(out=res[half], in_=res[half], func=ACT.Sigmoid)

        def finish_multiply(t):
            res = halves_of(result[t])
            for half in range(HALVES):
                nc.vector.tensor_mul(out=res[half], in0=res[half], in1=c_minus_h[(t, half)])

        def finish_add(t):
            res = halves_of(result[t])
            for half in range(HALVES):
                nc.vector.tensor_add(out=res[half], in0=res[half], in1=halves_of(h_sb[:, t, :])[half])
                store(t, half, res[half])

        c_minus_h = {}

        def open_c_minus_h(t):
            for half in range(HALVES):
                if C_LAST:
                    bank = turn_pool.tile([P, HALF], F32, name="turn")
                    nc.tensor.matmul(out=bank[:], lhsT=minus_one[:], rhs=halves_of(h_sb[:, t, :])[half], start=True, stop=False)
                    c_minus_h[(t, half)] = bank[:]
                else:
                    c_minus_h[(t, half)] = halves_of(c_minus_h_sb[:, t, :])[half]

        def close_c_minus_h(t):
            for half in range(HALVES):
                if C_LAST:
                    nc.tensor.matmul(
                        out=c_minus_h[(t, half)], lhsT=plus_one[:], rhs=halves_of(c_sb[:, t, :])[half], start=False, stop=True
                    )

        def store(t, half, src):
            nc.sync.dma_start(out=out[t * P : (t + 1) * P, half * HALF : (half + 1) * HALF], in_=src)

        def finish_blend(t, add_on_tensor):
            res = halves_of(result[t])
            for half in range(HALVES):
                nc.vector.tensor_mul(out=res[half], in0=res[half], in1=c_minus_h[(t, half)])
            for half in range(HALVES):
                if add_on_tensor:
                    bank = bank_of("blend", t, half, [P, HALF], F32)
                    nc.tensor.matmul(out=bank[:], lhsT=plus_one[:], rhs=halves_of(h_sb[:, t, :])[half], start=True, stop=False)
                    nc.tensor.matmul(out=bank[:], lhsT=identity[:], rhs=res[half], start=False, stop=True)
                    blended = keep.tile([P, HALF], F32, name="blended%d%d" % (t, half))
                    nc.scalar.copy(out=blended[:], in_=bank[:])
                    store(t, half, blended[:])
                elif ADD0_GPSIMD and t == 0:
                    nc.gpsimd.tensor_tensor(out=res[half], in0=res[half], in1=halves_of(h_sb[:, t, :])[half], op=ALU.add)
                    store(t, half, res[half])
                else:
                    nc.vector.tensor_add(out=res[half], in0=res[half], in1=halves_of(h_sb[:, t, :])[half])
                    store(t, half, res[half])

        zero_plane(w_plane)
        zero_plane(u_plane[0])
        nc.gpsimd.memset(minus_half[:], -0.5)
        nc.gpsimd.memset(spread_src[:].bitcast(F32), 0.0)
        make_identity(nc, identity[:])
        nc.gpsimd.memset(ones[:], 1.0)
        nc.gpsimd.tensor_copy(out=plus_one[:], in_=identity[:])
        nc.gpsimd.tensor_scalar(out=minus_one[:], in0=identity[:], scalar1=-1.0, scalar2=0.0, op0=ALU.mult, op1=ALU.add)
        nc.scalar.activation(out=table_warm[:], in_=minus_half[:], func=ACT.Sigmoid)

        load_activations(0)
        if HEAD == 0:
            load_activations(1)
            nc.sync.dma_start(out=spread_src[0:1, 0:2, :], in_=ln_gamma.unsqueeze(0))
            nc.sync.dma_start(out=spread_src[0:2, 2, :], in_=ln_beta)
            load_weights(0)
            load_activations(2)
            load_weights(1)
        else:
            nc.sync.dma_start(out=spread_src[0:1, 0:2, :], in_=ln_gamma.unsqueeze(0))
            nc.sync.dma_start(out=spread_src[0:2, 2, :], in_=ln_beta)
            load_weights(0)
            load_activations(1)
            load_weights(1)
            load_activations(2)
        sort_words(0)

        first_norm_step = 1
        blend_step = n_steps // 2
        for i in range(-1, n_steps - 1):
            if i + 4 < n_steps:
                load_activations(i + 4)
            if i + 3 < n_steps:
                load_weights(i + 3)
            if i + 3 == (n_steps - 1 if C_LAST else blend_step):
                nc.sync.dma_start(out=c_sb[:], in_=c.rearrange("(t p) k -> p t k", p=P))
            if HEAD == 2 and i == 1:
                multiply(steps[i], by_group=(U0_PIECES > 1))
            transpose(i + 1)
            regroup_and_quantise(i + 1)
            if i == -1:
                spread_constants()
            if i + 2 < n_steps:
                sort_words(i + 2)
            if 1 <= i + 2 < RUNS:
                zero_plane(u_plane[i + 2])
            if HEAD == 2 and i == 1:
                pass
            elif 0 <= i < n_steps - REGROUP:
                multiply(steps[i])
            elif i >= 0:
                multiply(steps[i][0:1])
            if i == 0:
                for half in range(HALVES):
                    for t in range(ROW_TILES):
                        nc.scalar.copy(out=halves_of(hidden_term[t])[half], in_=sums[("h", t, half)][:])
            if 0 <= i - first_norm_step < ROW_TILES:
                t = i - first_norm_step
                term = halves_of(hidden_term[t])
                mean, inv_std = statistics(term, "h%d" % t)
                scale_add(term, term, mean, inv_std, halves_of(gammas[:, 0, :]), halves_of(beta_sum))
            if i == blend_step and not C_LAST:
                nc.vector.tensor_sub(out=c_minus_h_sb[:], in0=c_sb[:], in1=h_sb[:])

        multiply(steps[n_steps - 1][0:1], by_group=True)
        finish_statistics(0)
        owed = [steps[s][1] for s in range(n_steps - REGROUP, n_steps)]
        multiply(owed)
        for t in range(ROW_TILES):
            open_c_minus_h(t)
            close_c_minus_h(t)
        if VTAIL == 0:
            finish_gate(0)
            finish_statistics(1)
            finish_gate(1)
            finish_blend(0, False)
            finish_blend(1, False)
        else:
            stats1 = keep.tile([P, HALVES, 6], F32, name="stats_x1")
            finish_centre(0)
            nc.vector.bn_stats(out=stats1[:, 0, :], in_=x_sums(1)[0])
            finish_sigmoid(0)
            nc.vector.bn_stats(out=stats1[:, 1, :], in_=x_sums(1)[1])
            x_stats[1] = aggregate(stats1, "x1")
            finish_centre(1)
            finish_multiply(0)
            finish_sigmoid(1)
            finish_add(0)
            finish_multiply(1)
            finish_add(1)
